import numpy as np
import ml_dtypes

BF16 = ml_dtypes.bfloat16


def bf(x):
    return np.asarray(x, np.float32).astype(BF16)


def f32(x):
    return np.asarray(x, np.float32)


def f64(x):
    return np.asarray(x).astype(np.float64)


def striped(idx):
    return np.tile(idx.reshape(-1, 16).T, (8, 1))


D, M, S, N, DEG = 128, 128, 2048, 1024, 16
GAIN = 1.414


def draw_mask():
    m = (np.random.random((N, S)) < DEG / S).astype(np.float32)
    m[np.arange(N), np.random.permutation(S)[:N]] = 1.0
    return bf(m)


def setup_inputs():
    sw = GAIN * np.sqrt(6.0 / (D + M))
    return {"table": bf(np.random.standard_normal((D, S))), "w2": bf(np.random.uniform(-sw, sw, (D, M))), "city_mask": draw_mask(), "prov_mask": draw_mask(), "offs": striped(np.random.permutation(S)[:N])}


def reference(table, w2, city_mask, prov_mask, offs):
    idx = offs[:16].T.reshape(-1)
    h = f64(w2).T @ f64(table)[:, idx]
    m3 = f64(city_mask)
    m4 = f64(prov_mask)
    att = m3 / m3.sum(axis=1, keepdims=True) + m4 / m4.sum(axis=1, keepdims=True)
    return h @ att

@@ -1,0 +1,91 @@
+import concourse.mybir as mybir
+from concourse.masks import make_identity
+
+BF16, F32, U16 = mybir.dt.bfloat16, mybir.dt.float32, mybir.dt.uint16
+MULT, ADD = mybir.AluOpType.mult, mybir.AluOpType.add
+COPY = mybir.ActivationFunctionType.Copy
+
+P = 128
+S = 2048
+N = 1024
+PIECE = 512
+BLOCKS = N // P
+BANKS = S // PIECE
+
+FLOPS = 2 * P * P * N + 2 * P * N * S
+
+
+def tile_ourslayer2_kernel(tc, table, w2, city_mask, prov_mask, offs, out):
+    nc = tc.nc
+    with (
+        tc.tile_pool(name="held", bufs=1) as held,
+        tc.tile_pool(name="mask_pool", bufs=BLOCKS) as mask_pool,
+        tc.tile_pool(name="work", bufs=2) as work,
+        tc.tile_pool(name="stats", bufs=4) as stats,
+        tc.psum_pool(name="psum_h", bufs=1) as psum_h,
+        tc.psum_pool(name="psum_out", bufs=1) as psum_out,
+    ):
+        offsets = held.tile([P, N // 16], U16, name="offsets")
+        nc.sync.dma_start(offsets[:], offs)
+        w2_sb = held.tile([P, P], BF16, name="w2_sb")
+        nc.sync.dma_start(w2_sb[:], w2)
+        table_sb = held.tile([P, S], BF16, name="table_sb")
+        nc.sync.dma_start(table_sb[:], table)
+        city_blocks, prov_blocks = [], []
+        for b in range(BLOCKS):
+            city = mask_pool.tile([P, S], BF16, name="city")
+            nc.sync.dma_start(city[:], city_mask[b * P : (b + 1) * P, :])
+            prov = mask_pool.tile([P, S], BF16, name="prov")
+            nc.sync.dma_start(prov[:], prov_mask[b * P : (b + 1) * P, :])
+            city_blocks.append(city)
+            prov_blocks.append(prov)
+
+        identity = held.tile([P, P], BF16, name="identity")
+        make_identity(nc, identity[:])
+
+        h_bf = held.tile([P, N], BF16, name="h_bf")
+        for piece in range(N // PIECE):
+            h_ps = psum_h.tile([P, PIECE], F32, name="h_ps")
+            piece_offsets = offsets[:, piece * (PIECE // 16) : (piece + 1) * (PIECE // 16)]
+            nc.tensor.matmul(h_ps[:], w2_sb[:], table_sb[:].indirect(piece_offsets), start=True, stop=True)
+            nc.vector.tensor_copy(h_bf[:, piece * PIECE : (piece + 1) * PIECE], h_ps[:])
+
+        hT_ps = psum_h.tile([P, N], BF16, name="hT_ps")
+        for b in range(BLOCKS):
+            nc.tensor.transpose(hT_ps[:, b * P : (b + 1) * P], h_bf[:, b * P : (b + 1) * P], identity[:])
+        hT = held.tile([P, N], BF16, name="hT")
+        nc.vector.tensor_copy(hT[:], hT_ps[:])
+
+        out_ps = [psum_out.tile([P, PIECE], F32, name=f"out_ps{c}") for c in range(BANKS)]
+        for b in range(BLOCKS):
+            city, prov = city_blocks[b], prov_blocks[b]
+            city_sum = stats.tile([P, 1], F32, name="city_sum")
+            city_copy = work.tile([P, S], BF16, name="city_copy")
+            nc.vector.tensor_scalar(city_copy[:], city[:], 1.0, None, MULT, ADD, accum_out=city_sum[:])
+            prov_sum = stats.tile([P, 1], F32, name="prov_sum")
+            prov_copy = work.tile([P, S], BF16, name="prov_copy")
+            nc.scalar.activation(prov_copy[:], prov[:], COPY, accum_out=prov_sum[:])
+            city_inv = stats.tile([P, 1], F32, name="city_inv")
+            nc.vector.reciprocal(city_inv[:], city_sum[:])
+            prov_inv = stats.tile([P, 1], F32, name="prov_inv")
+            nc.vector.reciprocal(prov_inv[:], prov_sum[:])
+
+            prov_att = work.tile([P, S], F32, name="prov_att")
+            nc.scalar.activation(prov_att[:], prov[:], COPY, scale=prov_inv[:])
+            att = work.tile([P, S], BF16, name="att")
+            nc.vector.scalar_tensor_tensor(att[:], city[:], city_inv[:], prov_att[:], MULT, ADD)
+
+            for c in range(BANKS):
+                nc.tensor.matmul(
+                    out_ps[c][:],
+                    hT[:, b * P : (b + 1) * P],
+                    att[:, c * PIECE : (c + 1) * PIECE],
+                    start=(b == 0),
+                    stop=(b == BLOCKS - 1),
+                )
+
+        out_sb = held.tile([P, S], F32, name="out_sb")
+        for c in range(BANKS):
+            columns = slice(c * PIECE, (c + 1) * PIECE)
+            nc.vector.tensor_copy(out_sb[:, columns], out_ps[c][:])
+            nc.sync.dma_start(out[:, columns], out_sb[:, columns])

@@ -4,6 +4,7 @@ from concourse.masks import make_identity
 BF16, F32, U16 = mybir.dt.bfloat16, mybir.dt.float32, mybir.dt.uint16
 MULT, ADD = mybir.AluOpType.mult, mybir.AluOpType.add
 COPY = mybir.ActivationFunctionType.Copy
+X = mybir.AxisListType.X
 
 P = 128
 S = 2048
@@ -11,6 +12,7 @@ N = 1024
 PIECE = 512
 BLOCKS = N // P
 BANKS = S // PIECE
+SLICES = S // P
 
 FLOPS = 2 * P * P * N + 2 * P * N * S
 
@@ -22,7 +24,7 @@ def tile_ourslayer2_kernel(tc, table, w2, city_mask, prov_mask, offs, out):
         tc.tile_pool(name="mask_pool", bufs=BLOCKS) as mask_pool,
         tc.tile_pool(name="work", bufs=2) as work,
         tc.tile_pool(name="stats", bufs=4) as stats,
-        tc.psum_pool(name="psum_h", bufs=1) as psum_h,
+        tc.psum_pool(name="psum_work", bufs=4) as psum_work,
         tc.psum_pool(name="psum_out", bufs=1) as psum_out,
     ):
         offsets = held.tile([P, N // 16], U16, name="offsets")
@@ -45,12 +47,12 @@ def tile_ourslayer2_kernel(tc, table, w2, city_mask, prov_mask, offs, out):
 
         h_bf = held.tile([P, N], BF16, name="h_bf")
         for piece in range(N // PIECE):
-            h_ps = psum_h.tile([P, PIECE], F32, name="h_ps")
+            h_ps = psum_work.tile([P, PIECE], F32, name="h_ps", tag="bank")
             piece_offsets = offsets[:, piece * (PIECE // 16) : (piece + 1) * (PIECE // 16)]
             nc.tensor.matmul(h_ps[:], w2_sb[:], table_sb[:].indirect(piece_offsets), start=True, stop=True)
             nc.vector.tensor_copy(h_bf[:, piece * PIECE : (piece + 1) * PIECE], h_ps[:])
 
-        hT_ps = psum_h.tile([P, N], BF16, name="hT_ps")
+        hT_ps = psum_work.tile([P, N], BF16, name="hT_ps", tag="bank")
         for b in range(BLOCKS):
             nc.tensor.transpose(hT_ps[:, b * P : (b + 1) * P], h_bf[:, b * P : (b + 1) * P], identity[:])
         hT = held.tile([P, N], BF16, name="hT")
@@ -59,21 +61,26 @@ def tile_ourslayer2_kernel(tc, table, w2, city_mask, prov_mask, offs, out):
         out_ps = [psum_out.tile([P, PIECE], F32, name=f"out_ps{c}") for c in range(BANKS)]
         for b in range(BLOCKS):
             city, prov = city_blocks[b], prov_blocks[b]
-            city_sum = stats.tile([P, 1], F32, name="city_sum")
-            city_copy = work.tile([P, S], BF16, name="city_copy")
-            nc.vector.tensor_scalar(city_copy[:], city[:], 1.0, None, MULT, ADD, accum_out=city_sum[:])
-            prov_sum = stats.tile([P, 1], F32, name="prov_sum")
-            prov_copy = work.tile([P, S], BF16, name="prov_copy")
-            nc.scalar.activation(prov_copy[:], prov[:], COPY, accum_out=prov_sum[:])
-            city_inv = stats.tile([P, 1], F32, name="city_inv")
-            nc.vector.reciprocal(city_inv[:], city_sum[:])
-            prov_inv = stats.tile([P, 1], F32, name="prov_inv")
-            nc.vector.reciprocal(prov_inv[:], prov_sum[:])
+
+            folded = psum_work.tile([P, 2, P], F32, name="folded", tag="bank")
+            for which, mask in enumerate((city, prov)):
+                for s in range(SLICES):
+                    nc.tensor.matmul(
+                        folded[:, which, :],
+                        identity[:],
+                        mask[:, s * P : (s + 1) * P],
+                        start=(s == 0),
+                        stop=(s == SLICES - 1),
+                    )
+            sums = stats.tile([P, 2], F32, name="sums")
+            nc.vector.tensor_reduce(sums[:], folded[:], X, ADD)
+            inv = stats.tile([P, 2], F32, name="inv")
+            nc.vector.reciprocal(inv[:], sums[:])
 
             prov_att = work.tile([P, S], F32, name="prov_att")
-            nc.scalar.activation(prov_att[:], prov[:], COPY, scale=prov_inv[:])
+            nc.scalar.activation(prov_att[:], prov[:], COPY, scale=inv[:, 1:2])
             att = work.tile([P, S], BF16, name="att")
-            nc.vector.scalar_tensor_tensor(att[:], city[:], city_inv[:], prov_att[:], MULT, ADD)
+            nc.vector.scalar_tensor_tensor(att[:], city[:], inv[:, 0:1], prov_att[:], MULT, ADD)
 
             for c in range(BANKS):
                 nc.tensor.matmul(
@@ -87,5 +94,8 @@ def tile_ourslayer2_kernel(tc, table, w2, city_mask, prov_mask, offs, out):
         out_sb = held.tile([P, S], F32, name="out_sb")
         for c in range(BANKS):
             columns = slice(c * PIECE, (c + 1) * PIECE)
-            nc.vector.tensor_copy(out_sb[:, columns], out_ps[c][:])
+            if c % 2 == 0:
+                nc.vector.tensor_copy(out_sb[:, columns], out_ps[c][:])
+            else:
+                nc.scalar.copy(out_sb[:, columns], out_ps[c][:])
             nc.sync.dma_start(out[:, columns], out_sb[:, columns])

@@ -12,6 +12,7 @@ N = 1024
 PIECE = 512
 BLOCKS = N // P
 BANKS = S // PIECE
+HALF = S // 2
 SLICES = S // P
 
 FLOPS = 2 * P * P * N + 2 * P * N * S
@@ -30,9 +31,7 @@ def tile_ourslayer2_kernel(tc, table, w2, city_mask, prov_mask, offs, out):
         offsets = held.tile([P, N // 16], U16, name="offsets")
         nc.sync.dma_start(offsets[:], offs)
         w2_sb = held.tile([P, P], BF16, name="w2_sb")
-        nc.sync.dma_start(w2_sb[:], w2)
         table_sb = held.tile([P, S], BF16, name="table_sb")
-        nc.sync.dma_start(table_sb[:], table)
         city_blocks, prov_blocks = [], []
         for b in range(BLOCKS):
             city = mask_pool.tile([P, S], BF16, name="city")
@@ -41,9 +40,31 @@ def tile_ourslayer2_kernel(tc, table, w2, city_mask, prov_mask, offs, out):
             nc.sync.dma_start(prov[:], prov_mask[b * P : (b + 1) * P, :])
             city_blocks.append(city)
             prov_blocks.append(prov)
+            if b == 0:
+                nc.sync.dma_start(w2_sb[:], w2)
+                nc.sync.dma_start(table_sb[:], table)
 
         identity = held.tile([P, P], BF16, name="identity")
         make_identity(nc, identity[:])
+
+        def inverse_row_sums(b):
+            folded = psum_work.tile([P, 2, P], F32, name="folded", tag="bank")
+            for which, mask in enumerate((city_blocks[b], prov_blocks[b])):
+                for s in range(SLICES):
+                    nc.tensor.matmul(
+                        folded[:, which, :],
+                        identity[:],
+                        mask[:, s * P : (s + 1) * P],
+                        start=(s == 0),
+                        stop=(s == SLICES - 1),
+                    )
+            sums = stats.tile([P, 2], F32, name="sums")
+            nc.vector.tensor_reduce(sums[:], folded[:], X, ADD)
+            inv = stats.tile([P, 2], F32, name="inv", bufs=BLOCKS)
+            nc.vector.reciprocal(inv[:], sums[:])
+            return inv
+
+        inv_blocks = [inverse_row_sums(0)]
 
         h_bf = held.tile([P, N], BF16, name="h_bf")
         for piece in range(N // PIECE):
@@ -58,38 +79,26 @@ def tile_ourslayer2_kernel(tc, table, w2, city_mask, prov_mask, offs, out):
         hT = held.tile([P, N], BF16, name="hT")
         nc.vector.tensor_copy(hT[:], hT_ps[:])
 
+        inv_blocks += [inverse_row_sums(b) for b in range(1, BLOCKS)]
+
         out_ps = [psum_out.tile([P, PIECE], F32, name=f"out_ps{c}") for c in range(BANKS)]
         for b in range(BLOCKS):
-            city, prov = city_blocks[b], prov_blocks[b]
+            city, prov, inv = city_blocks[b], prov_blocks[b], inv_blocks[b]
 
-            folded = psum_work.tile([P, 2, P], F32, name="folded", tag="bank")
-            for which, mask in enumerate((city, prov)):
-                for s in range(SLICES):
+            for half in range(S // HALF):
+                columns = slice(half * HALF, (half + 1) * HALF)
+                prov_att = work.tile([P, HALF], F32, name="prov_att", bufs=4)
+                nc.scalar.activation(prov_att[:], prov[:, columns], COPY, scale=inv[:, 1:2])
+                att = work.tile([P, HALF], BF16, name="att", bufs=2 * BLOCKS)
+                nc.vector.scalar_tensor_tensor(att[:], city[:, columns], inv[:, 0:1], prov_att[:], MULT, ADD)
+                for k in range(HALF // PIECE):
                     nc.tensor.matmul(
-                        folded[:, which, :],
-                        identity[:],
-                        mask[:, s * P : (s + 1) * P],
-                        start=(s == 0),
-                        stop=(s == SLICES - 1),
+                        out_ps[half * (HALF // PIECE) + k][:],
+                        hT[:, b * P : (b + 1) * P],
+                        att[:, k * PIECE : (k + 1) * PIECE],
+                        start=(b == 0),
+                        stop=(b == BLOCKS - 1),
                     )
-            sums = stats.tile([P, 2], F32, name="sums")
-            nc.vector.tensor_reduce(sums[:], folded[:], X, ADD)
-            inv = stats.tile([P, 2], F32, name="inv")
-            nc.vector.reciprocal(inv[:], sums[:])
-
-            prov_att = work.tile([P, S], F32, name="prov_att")
-            nc.scalar.activation(prov_att[:], prov[:], COPY, scale=inv[:, 1:2])
-            att = work.tile([P, S], BF16, name="att")
-            nc.vector.scalar_tensor_tensor(att[:], city[:], inv[:, 0:1], prov_att[:], MULT, ADD)
-
-            for c in range(BANKS):
-                nc.tensor.matmul(
-                    out_ps[c][:],
-                    hT[:, b * P : (b + 1) * P],
-                    att[:, c * PIECE : (c + 1) * PIECE],
-                    start=(b == 0),
-                    stop=(b == BLOCKS - 1),
-                )
 
         out_sb = held.tile([P, S], F32, name="out_sb")
         for c in range(BANKS):

@@ -4,7 +4,6 @@ from concourse.masks import make_identity
 BF16, F32, U16 = mybir.dt.bfloat16, mybir.dt.float32, mybir.dt.uint16
 MULT, ADD = mybir.AluOpType.mult, mybir.AluOpType.add
 COPY = mybir.ActivationFunctionType.Copy
-X = mybir.AxisListType.X
 
 P = 128
 S = 2048
@@ -12,8 +11,6 @@ N = 1024
 PIECE = 512
 BLOCKS = N // P
 BANKS = S // PIECE
-HALF = S // 2
-SLICES = S // P
 
 FLOPS = 2 * P * P * N + 2 * P * N * S
 
@@ -23,15 +20,17 @@ def tile_ourslayer2_kernel(tc, table, w2, city_mask, prov_mask, offs, out):
     with (
         tc.tile_pool(name="held", bufs=1) as held,
         tc.tile_pool(name="mask_pool", bufs=BLOCKS) as mask_pool,
-        tc.tile_pool(name="work", bufs=2) as work,
-        tc.tile_pool(name="stats", bufs=4) as stats,
-        tc.psum_pool(name="psum_work", bufs=4) as psum_work,
+        tc.tile_pool(name="work", bufs=3) as work,
+        tc.tile_pool(name="stats", bufs=BLOCKS) as stats,
+        tc.psum_pool(name="psum_work", bufs=2) as psum_work,
         tc.psum_pool(name="psum_out", bufs=1) as psum_out,
     ):
         offsets = held.tile([P, N // 16], U16, name="offsets")
         nc.sync.dma_start(offsets[:], offs)
         w2_sb = held.tile([P, P], BF16, name="w2_sb")
+        nc.sync.dma_start(w2_sb[:], w2)
         table_sb = held.tile([P, S], BF16, name="table_sb")
+        nc.sync.dma_start(table_sb[:], table)
         city_blocks, prov_blocks = [], []
         for b in range(BLOCKS):
             city = mask_pool.tile([P, S], BF16, name="city")
@@ -40,31 +39,9 @@ def tile_ourslayer2_kernel(tc, table, w2, city_mask, prov_mask, offs, out):
             nc.sync.dma_start(prov[:], prov_mask[b * P : (b + 1) * P, :])
             city_blocks.append(city)
             prov_blocks.append(prov)
-            if b == 0:
-                nc.sync.dma_start(w2_sb[:], w2)
-                nc.sync.dma_start(table_sb[:], table)
 
         identity = held.tile([P, P], BF16, name="identity")
         make_identity(nc, identity[:])
-
-        def inverse_row_sums(b):
-            folded = psum_work.tile([P, 2, P], F32, name="folded", tag="bank")
-            for which, mask in enumerate((city_blocks[b], prov_blocks[b])):
-                for s in range(SLICES):
-                    nc.tensor.matmul(
-                        folded[:, which, :],
-                        identity[:],
-                        mask[:, s * P : (s + 1) * P],
-                        start=(s == 0),
-                        stop=(s == SLICES - 1),
-                    )
-            sums = stats.tile([P, 2], F32, name="sums")
-            nc.vector.tensor_reduce(sums[:], folded[:], X, ADD)
-            inv = stats.tile([P, 2], F32, name="inv", bufs=BLOCKS)
-            nc.vector.reciprocal(inv[:], sums[:])
-            return inv
-
-        inv_blocks = [inverse_row_sums(0)]
 
         h_bf = held.tile([P, N], BF16, name="h_bf")
         for piece in range(N // PIECE):
@@ -79,25 +56,29 @@ def tile_ourslayer2_kernel(tc, table, w2, city_mask, prov_mask, offs, out):
         hT = held.tile([P, N], BF16, name="hT")
         nc.vector.tensor_copy(hT[:], hT_ps[:])
 
-        inv_blocks += [inverse_row_sums(b) for b in range(1, BLOCKS)]
-
         out_ps = [psum_out.tile([P, PIECE], F32, name=f"out_ps{c}") for c in range(BANKS)]
         for b in range(BLOCKS):
-            city, prov, inv = city_blocks[b], prov_blocks[b], inv_blocks[b]
+            city, prov = city_blocks[b], prov_blocks[b]
 
-            for half in range(S // HALF):
-                columns = slice(half * HALF, (half + 1) * HALF)
-                prov_att = work.tile([P, HALF], F32, name="prov_att", bufs=4)
-                nc.scalar.activation(prov_att[:], prov[:, columns], COPY, scale=inv[:, 1:2])
-                att = work.tile([P, HALF], BF16, name="att", bufs=2 * BLOCKS)
-                nc.vector.scalar_tensor_tensor(att[:], city[:, columns], inv[:, 0:1], prov_att[:], MULT, ADD)
-                for k in range(HALF // PIECE):
+            city_pass = work.tile([P, S], BF16, name="city_pass", bufs=2)
+            city_sum = stats.tile([P, 1], F32, name="city_sum")
+            nc.vector.tensor_scalar(city_pass[:], city[:], 1.0, None, MULT, ADD, accum_out=city_sum[:])
+            prov_pass = work.tile([P, S], BF16, name="prov_pass", bufs=2)
+            prov_sum = stats.tile([P, 1], F32, name="prov_sum")
+            nc.scalar.activation(prov_pass[:], prov[:], COPY, accum_out=prov_sum[:])
+
+            for which, (name, mask, total) in enumerate((("city", city, city_sum), ("prov", prov, prov_sum))):
+                inv = stats.tile([P, 1], F32, name=name + "_inv")
+                nc.vector.reciprocal(inv[:], total[:])
+                scaled = work.tile([P, P], BF16, name=name + "_scaled")
+                nc.vector.tensor_scalar(scaled[:], hT[:, b * P : (b + 1) * P], inv[:], None, MULT)
+                for c in range(BANKS):
                     nc.tensor.matmul(
-                        out_ps[half * (HALF // PIECE) + k][:],
-                        hT[:, b * P : (b + 1) * P],
-                        att[:, k * PIECE : (k + 1) * PIECE],
-                        start=(b == 0),
-                        stop=(b == BLOCKS - 1),
+                        out_ps[c][:],
+                        scaled[:],
+                        mask[:, c * PIECE : (c + 1) * PIECE],
+                        start=(b == 0 and which == 0),
+                        stop=(b == BLOCKS - 1 and which == 1),
                     )
 
         out_sb = held.tile([P, S], F32, name="out_sb")

@@ -22,8 +22,8 @@ def tile_ourslayer2_kernel(tc, table, w2, city_mask, prov_mask, offs, out):
         tc.tile_pool(name="mask_pool", bufs=BLOCKS) as mask_pool,
         tc.tile_pool(name="work", bufs=3) as work,
         tc.tile_pool(name="stats", bufs=BLOCKS) as stats,
-        tc.psum_pool(name="psum_work", bufs=2) as psum_work,
-        tc.psum_pool(name="psum_out", bufs=1) as psum_out,
+        tc.psum_pool(name="psum_h", bufs=N // PIECE) as psum_h,
+        tc.psum_pool(name="psum_held", bufs=1) as psum_held,
     ):
         offsets = held.tile([P, N // 16], U16, name="offsets")
         nc.sync.dma_start(offsets[:], offs)
@@ -43,20 +43,19 @@ def tile_ourslayer2_kernel(tc, table, w2, city_mask, prov_mask, offs, out):
         identity = held.tile([P, P], BF16, name="identity")
         make_identity(nc, identity[:])
 
-        h_bf = held.tile([P, N], BF16, name="h_bf")
+        hT_blocks = []
         for piece in range(N // PIECE):
-            h_ps = psum_work.tile([P, PIECE], F32, name="h_ps", tag="bank")
+            h_ps = psum_h.tile([P, PIECE], F32, name="h_ps")
             piece_offsets = offsets[:, piece * (PIECE // 16) : (piece + 1) * (PIECE // 16)]
             nc.tensor.matmul(h_ps[:], w2_sb[:], table_sb[:].indirect(piece_offsets), start=True, stop=True)
-            nc.vector.tensor_copy(h_bf[:, piece * PIECE : (piece + 1) * PIECE], h_ps[:])
+            h_bf = held.tile([P, PIECE], BF16, name=f"h_bf{piece}")
+            nc.scalar.copy(h_bf[:], h_ps[:])
+            hT_ps = psum_held.tile([P, PIECE], BF16, name=f"hT_ps{piece}")
+            for k in range(PIECE // P):
+                nc.tensor.transpose(hT_ps[:, k * P : (k + 1) * P], h_bf[:, k * P : (k + 1) * P], identity[:])
+                hT_blocks.append(hT_ps[:, k * P : (k + 1) * P])
 
-        hT_ps = psum_work.tile([P, N], BF16, name="hT_ps", tag="bank")
-        for b in range(BLOCKS):
-            nc.tensor.transpose(hT_ps[:, b * P : (b + 1) * P], h_bf[:, b * P : (b + 1) * P], identity[:])
-        hT = held.tile([P, N], BF16, name="hT")
-        nc.vector.tensor_copy(hT[:], hT_ps[:])
-
-        out_ps = [psum_out.tile([P, PIECE], F32, name=f"out_ps{c}") for c in range(BANKS)]
+        out_ps = [psum_held.tile([P, PIECE], F32, name=f"out_ps{c}") for c in range(BANKS)]
         for b in range(BLOCKS):
             city, prov = city_blocks[b], prov_blocks[b]
 
@@ -71,7 +70,7 @@ def tile_ourslayer2_kernel(tc, table, w2, city_mask, prov_mask, offs, out):
                 inv = stats.tile([P, 1], F32, name=name + "_inv")
                 nc.vector.reciprocal(inv[:], total[:])
                 scaled = work.tile([P, P], BF16, name=name + "_scaled")
-                nc.vector.tensor_scalar(scaled[:], hT[:, b * P : (b + 1) * P], inv[:], None, MULT)
+                nc.vector.tensor_scalar(scaled[:], hT_blocks[b], inv[:], None, MULT)
                 for c in range(BANKS):
                     nc.tensor.matmul(
                         out_ps[c][:],

@@ -59,14 +59,15 @@ def tile_ourslayer2_kernel(tc, table, w2, city_mask, prov_mask, offs, out):
         for b in range(BLOCKS):
             city, prov = city_blocks[b], prov_blocks[b]
 
-            city_pass = work.tile([P, S], BF16, name="city_pass", bufs=2)
-            city_sum = stats.tile([P, 1], F32, name="city_sum")
-            nc.vector.tensor_scalar(city_pass[:], city[:], 1.0, None, MULT, ADD, accum_out=city_sum[:])
-            prov_pass = work.tile([P, S], BF16, name="prov_pass", bufs=2)
-            prov_sum = stats.tile([P, 1], F32, name="prov_sum")
-            nc.scalar.activation(prov_pass[:], prov[:], COPY, accum_out=prov_sum[:])
+            for which, (name, mask) in enumerate((("city", city), ("prov", prov))):
+                total = stats.tile([P, 1], F32, name=name + "_total")
+                if (2 * b + which) % 3 == 1:
+                    scalar_pass = work.tile([P, S], BF16, name="scalar_pass", bufs=2)
+                    nc.scalar.activation(scalar_pass[:], mask[:], COPY, accum_out=total[:])
+                else:
+                    vector_pass = work.tile([P, S], BF16, name="vector_pass", bufs=2)
+                    nc.vector.tensor_scalar(vector_pass[:], mask[:], 1.0, None, MULT, ADD, accum_out=total[:])
 
-            for which, (name, mask, total) in enumerate((("city", city, city_sum), ("prov", prov, prov_sum))):
                 inv = stats.tile([P, 1], F32, name=name + "_inv")
                 nc.vector.reciprocal(inv[:], total[:])
                 scaled = work.tile([P, P], BF16, name=name + "_scaled")

@@ -11,6 +11,7 @@ N = 1024
 PIECE = 512
 BLOCKS = N // P
 BANKS = S // PIECE
+LATE = 2
 
 FLOPS = 2 * P * P * N + 2 * P * N * S
 
@@ -55,37 +56,42 @@ def tile_ourslayer2_kernel(tc, table, w2, city_mask, prov_mask, offs, out):
                 nc.tensor.transpose(hT_ps[:, k * P : (k + 1) * P], h_bf[:, k * P : (k + 1) * P], identity[:])
                 hT_blocks.append(hT_ps[:, k * P : (k + 1) * P])
 
+        def weights_of(b, which, name):
+            mask = (city_blocks, prov_blocks)[which][b]
+            total = stats.tile([P, 1], F32, name=name + "_total")
+            if (2 * b + which) % 3 == 1:
+                scalar_pass = work.tile([P, S], BF16, name="scalar_pass", bufs=2)
+                nc.scalar.activation(scalar_pass[:], mask[:], COPY, accum_out=total[:])
+            else:
+                vector_pass = work.tile([P, S], BF16, name="vector_pass", bufs=2)
+                nc.vector.tensor_scalar(vector_pass[:], mask[:], 1.0, None, MULT, ADD, accum_out=total[:])
+            inv = stats.tile([P, 1], F32, name=name + "_inv")
+            nc.vector.reciprocal(inv[:], total[:])
+            scaled = work.tile([P, P], BF16, name=name + "_scaled")
+            nc.vector.tensor_scalar(scaled[:], hT_blocks[b], inv[:], None, MULT)
+            return scaled, mask
+
         out_ps = [psum_held.tile([P, PIECE], F32, name=f"out_ps{c}") for c in range(BANKS)]
-        for b in range(BLOCKS):
-            city, prov = city_blocks[b], prov_blocks[b]
-
-            for which, (name, mask) in enumerate((("city", city), ("prov", prov))):
-                total = stats.tile([P, 1], F32, name=name + "_total")
-                if (2 * b + which) % 3 == 1:
-                    scalar_pass = work.tile([P, S], BF16, name="scalar_pass", bufs=2)
-                    nc.scalar.activation(scalar_pass[:], mask[:], COPY, accum_out=total[:])
-                else:
-                    vector_pass = work.tile([P, S], BF16, name="vector_pass", bufs=2)
-                    nc.vector.tensor_scalar(vector_pass[:], mask[:], 1.0, None, MULT, ADD, accum_out=total[:])
-
-                inv = stats.tile([P, 1], F32, name=name + "_inv")
-                nc.vector.reciprocal(inv[:], total[:])
-                scaled = work.tile([P, P], BF16, name=name + "_scaled")
-                nc.vector.tensor_scalar(scaled[:], hT_blocks[b], inv[:], None, MULT)
+        for b in range(BLOCKS - LATE):
+            for which, name in enumerate(("city", "prov")):
+                scaled, mask = weights_of(b, which, name)
                 for c in range(BANKS):
                     nc.tensor.matmul(
-                        out_ps[c][:],
-                        scaled[:],
-                        mask[:, c * PIECE : (c + 1) * PIECE],
-                        start=(b == 0 and which == 0),
-                        stop=(b == BLOCKS - 1 and which == 1),
+                        out_ps[c][:], scaled[:], mask[:, c * PIECE : (c + 1) * PIECE], start=(b == 0 and which == 0), stop=False
                     )
 
+        late = [
+            weights_of(b, which, name)
+            for b in range(BLOCKS - LATE, BLOCKS)
+            for which, name in enumerate(("city", "prov"))
+        ]
         out_sb = held.tile([P, S], F32, name="out_sb")
         for c in range(BANKS):
             columns = slice(c * PIECE, (c + 1) * PIECE)
+            for k, (scaled, mask) in enumerate(late):
+                nc.tensor.matmul(out_ps[c][:], scaled[:], mask[:, columns], start=False, stop=(k == len(late) - 1))
             if c % 2 == 0:
-                nc.vector.tensor_copy(out_sb[:, columns], out_ps[c][:])
-            else:
                 nc.scalar.copy(out_sb[:, columns], out_ps[c][:])
+            else:
+                nc.vector.tensor_copy(out_sb[:, columns], out_ps[c][:])
             nc.sync.dma_start(out[:, columns], out_sb[:, columns])

@@ -59,7 +59,7 @@ def tile_ourslayer2_kernel(tc, table, w2, city_mask, prov_mask, offs, out):
         def weights_of(b, which, name):
             mask = (city_blocks, prov_blocks)[which][b]
             total = stats.tile([P, 1], F32, name=name + "_total")
-            if (2 * b + which) % 3 == 1:
+            if (2 * b + which) % 3 == 2:
                 scalar_pass = work.tile([P, S], BF16, name="scalar_pass", bufs=2)
                 nc.scalar.activation(scalar_pass[:], mask[:], COPY, accum_out=total[:])
             else:

@@ -11,7 +11,7 @@ N = 1024
 PIECE = 512
 BLOCKS = N // P
 BANKS = S // PIECE
-LATE = 2
+LATE = 1
 
 FLOPS = 2 * P * P * N + 2 * P * N * S
 

@@ -59,7 +59,7 @@ def tile_ourslayer2_kernel(tc, table, w2, city_mask, prov_mask, offs, out):
         def weights_of(b, which, name):
             mask = (city_blocks, prov_blocks)[which][b]
             total = stats.tile([P, 1], F32, name=name + "_total")
-            if (2 * b + which) % 3 == 2:
+            if (2 * b + which) % 5 in (2, 4):
                 scalar_pass = work.tile([P, S], BF16, name="scalar_pass", bufs=2)
                 nc.scalar.activation(scalar_pass[:], mask[:], COPY, accum_out=total[:])
             else:

@@ -8,9 +8,10 @@ COPY = mybir.ActivationFunctionType.Copy
 P = 128
 S = 2048
 N = 1024
-PIECE = 512
+BANK = 512
 BLOCKS = N // P
-BANKS = S // PIECE
+BANKS = S // BANK
+PIECES = (1, 3, 4)
 LATE = 1
 
 FLOPS = 2 * P * P * N + 2 * P * N * S
@@ -23,7 +24,7 @@ def tile_ourslayer2_kernel(tc, table, w2, city_mask, prov_mask, offs, out):
         tc.tile_pool(name="mask_pool", bufs=BLOCKS) as mask_pool,
         tc.tile_pool(name="work", bufs=3) as work,
         tc.tile_pool(name="stats", bufs=BLOCKS) as stats,
-        tc.psum_pool(name="psum_h", bufs=N // PIECE) as psum_h,
+        tc.psum_pool(name="psum_h", bufs=2) as psum_h,
         tc.psum_pool(name="psum_held", bufs=1) as psum_held,
     ):
         offsets = held.tile([P, N // 16], U16, name="offsets")
@@ -35,7 +36,12 @@ def tile_ourslayer2_kernel(tc, table, w2, city_mask, prov_mask, offs, out):
         city_blocks, prov_blocks = [], []
         for b in range(BLOCKS):
             city = mask_pool.tile([P, S], BF16, name="city")
-            nc.sync.dma_start(city[:], city_mask[b * P : (b + 1) * P, :])
+            if b == 0:
+                for half in range(2):
+                    columns = slice(half * (S // 2), (half + 1) * (S // 2))
+                    nc.sync.dma_start(city[:, columns], city_mask[0:P, columns])
+            else:
+                nc.sync.dma_start(city[:], city_mask[b * P : (b + 1) * P, :])
             prov = mask_pool.tile([P, S], BF16, name="prov")
             nc.sync.dma_start(prov[:], prov_mask[b * P : (b + 1) * P, :])
             city_blocks.append(city)
@@ -45,21 +51,36 @@ def tile_ourslayer2_kernel(tc, table, w2, city_mask, prov_mask, offs, out):
         make_identity(nc, identity[:])
 
         hT_blocks = []
-        for piece in range(N // PIECE):
-            h_ps = psum_h.tile([P, PIECE], F32, name="h_ps")
-            piece_offsets = offsets[:, piece * (PIECE // 16) : (piece + 1) * (PIECE // 16)]
-            nc.tensor.matmul(h_ps[:], w2_sb[:], table_sb[:].indirect(piece_offsets), start=True, stop=True)
-            h_bf = held.tile([P, PIECE], BF16, name=f"h_bf{piece}")
-            nc.scalar.copy(h_bf[:], h_ps[:])
-            hT_ps = psum_held.tile([P, PIECE], BF16, name=f"hT_ps{piece}")
-            for k in range(PIECE // P):
+        for piece, count in enumerate(PIECES):
+            first = len(hT_blocks)
+            width = count * P
+            h_ps = psum_h.tile([P, BANK], F32, name="h_ps", tag="h_ps")
+            piece_offsets = offsets[:, first * (P // 16) : (first + count) * (P // 16)]
+            nc.tensor.matmul(h_ps[:, 0:width], w2_sb[:], table_sb[:].indirect(piece_offsets), start=True, stop=True)
+            h_bf = held.tile([P, width], BF16, name=f"h_bf{piece}")
+            nc.scalar.copy(h_bf[:], h_ps[:, 0:width])
+            if piece < len(PIECES) - 1:
+                hT_ps = psum_held.tile([P, width], BF16, name=f"hT_ps{piece}")
+            else:
+                hT_ps = psum_h.tile([P, width], BF16, name="hT_ps", tag="h_ps")
+            for k in range(count):
                 nc.tensor.transpose(hT_ps[:, k * P : (k + 1) * P], h_bf[:, k * P : (k + 1) * P], identity[:])
                 hT_blocks.append(hT_ps[:, k * P : (k + 1) * P])
 
         def weights_of(b, which, name):
             mask = (city_blocks, prov_blocks)[which][b]
             total = stats.tile([P, 1], F32, name=name + "_total")
-            if (2 * b + which) % 5 in (2, 4):
+            if b == 0 and which == 0:
+                vector_pass = work.tile([P, S], BF16, name="vector_pass", bufs=2)
+                half_total = stats.tile([P, 1], F32, name="half_total")
+                left, right = slice(0, S // 2), slice(S // 2, S)
+                nc.vector.tensor_scalar(
+                    vector_pass[:, left], mask[:, left], 1.0, None, MULT, ADD, accum_out=half_total[:]
+                )
+                nc.vector.tensor_scalar(
+                    vector_pass[:, right], mask[:, right], 1.0, half_total[:], MULT, ADD, accum_out=total[:]
+                )
+            elif which == 0:
                 scalar_pass = work.tile([P, S], BF16, name="scalar_pass", bufs=2)
                 nc.scalar.activation(scalar_pass[:], mask[:], COPY, accum_out=total[:])
             else:
@@ -71,13 +92,13 @@ def tile_ourslayer2_kernel(tc, table, w2, city_mask, prov_mask, offs, out):
             nc.vector.tensor_scalar(scaled[:], hT_blocks[b], inv[:], None, MULT)
             return scaled, mask
 
-        out_ps = [psum_held.tile([P, PIECE], F32, name=f"out_ps{c}") for c in range(BANKS)]
+        out_ps = [psum_held.tile([P, BANK], F32, name=f"out_ps{c}") for c in range(BANKS)]
         for b in range(BLOCKS - LATE):
             for which, name in enumerate(("city", "prov")):
                 scaled, mask = weights_of(b, which, name)
                 for c in range(BANKS):
                     nc.tensor.matmul(
-                        out_ps[c][:], scaled[:], mask[:, c * PIECE : (c + 1) * PIECE], start=(b == 0 and which == 0), stop=False
+                        out_ps[c][:], scaled[:], mask[:, c * BANK : (c + 1) * BANK], start=(b == 0 and which == 0), stop=False
                     )
 
         late = [
@@ -87,7 +108,7 @@ def tile_ourslayer2_kernel(tc, table, w2, city_mask, prov_mask, offs, out):
         ]
         out_sb = held.tile([P, S], F32, name="out_sb")
         for c in range(BANKS):
-            columns = slice(c * PIECE, (c + 1) * PIECE)
+            columns = slice(c * BANK, (c + 1) * BANK)
             for k, (scaled, mask) in enumerate(late):
                 nc.tensor.matmul(out_ps[c][:], scaled[:], mask[:, columns], start=False, stop=(k == len(late) - 1))
             if c % 2 == 0:

@@ -27,12 +27,12 @@ def tile_ourslayer2_kernel(tc, table, w2, city_mask, prov_mask, offs, out):
         tc.psum_pool(name="psum_h", bufs=2) as psum_h,
         tc.psum_pool(name="psum_held", bufs=1) as psum_held,
     ):
-        offsets = held.tile([P, N // 16], U16, name="offsets")
-        nc.sync.dma_start(offsets[:], offs)
-        w2_sb = held.tile([P, P], BF16, name="w2_sb")
-        nc.sync.dma_start(w2_sb[:], w2)
         table_sb = held.tile([P, S], BF16, name="table_sb")
         nc.sync.dma_start(table_sb[:], table)
+        w2_sb = held.tile([P, P], BF16, name="w2_sb")
+        nc.scalar.dma_start(w2_sb[:], w2)
+        offsets = held.tile([P, N // 16], U16, name="offsets")
+        nc.sync.dma_start(offsets[:], offs)
         city_blocks, prov_blocks = [], []
         for b in range(BLOCKS):
             city = mask_pool.tile([P, S], BF16, name="city")
@@ -70,26 +70,29 @@ def tile_ourslayer2_kernel(tc, table, w2, city_mask, prov_mask, offs, out):
         def weights_of(b, which, name):
             mask = (city_blocks, prov_blocks)[which][b]
             total = stats.tile([P, 1], F32, name=name + "_total")
-            if b == 0 and which == 0:
-                vector_pass = work.tile([P, S], BF16, name="vector_pass", bufs=2)
-                half_total = stats.tile([P, 1], F32, name="half_total")
-                left, right = slice(0, S // 2), slice(S // 2, S)
-                nc.vector.tensor_scalar(
-                    vector_pass[:, left], mask[:, left], 1.0, None, MULT, ADD, accum_out=half_total[:]
-                )
-                nc.vector.tensor_scalar(
-                    vector_pass[:, right], mask[:, right], 1.0, half_total[:], MULT, ADD, accum_out=total[:]
-                )
-            elif which == 0:
+            if which == 0 and b > 0:
                 scalar_pass = work.tile([P, S], BF16, name="scalar_pass", bufs=2)
                 nc.scalar.activation(scalar_pass[:], mask[:], COPY, accum_out=total[:])
+                scalar_inv = stats.tile([P, 1], F32, name="scalar_inv")
+                inv = scalar_inv[:]
             else:
-                vector_pass = work.tile([P, S], BF16, name="vector_pass", bufs=2)
-                nc.vector.tensor_scalar(vector_pass[:], mask[:], 1.0, None, MULT, ADD, accum_out=total[:])
-            inv = stats.tile([P, 1], F32, name=name + "_inv")
-            nc.vector.reciprocal(inv[:], total[:])
+                vector_tile = work.tile([P, S // 2 + 1], F32, name="vector_tile", bufs=2)
+                unused = vector_tile[:, 0 : S // 2].bitcast(BF16)
+                inv = vector_tile[:, S // 2 : S // 2 + 1]
+                if b == 0 and which == 0:
+                    half_total = stats.tile([P, 1], F32, name="half_total")
+                    left, right = slice(0, S // 2), slice(S // 2, S)
+                    nc.vector.tensor_scalar(
+                        unused[:, left], mask[:, left], 1.0, None, MULT, ADD, accum_out=half_total[:]
+                    )
+                    nc.vector.tensor_scalar(
+                        unused[:, right], mask[:, right], 1.0, half_total[:], MULT, ADD, accum_out=total[:]
+                    )
+                else:
+                    nc.vector.tensor_scalar(unused, mask[:], 1.0, None, MULT, ADD, accum_out=total[:])
+            nc.vector.reciprocal(inv, total[:])
             scaled = work.tile([P, P], BF16, name=name + "_scaled")
-            nc.vector.tensor_scalar(scaled[:], hT_blocks[b], inv[:], None, MULT)
+            nc.vector.tensor_scalar(scaled[:], hT_blocks[b], inv, None, MULT)
             return scaled, mask
 
         out_ps = [psum_held.tile([P, BANK], F32, name=f"out_ps{c}") for c in range(BANKS)]

@@ -12,7 +12,7 @@ BANK = 512
 BLOCKS = N // P
 BANKS = S // BANK
 PIECES = (1, 3, 4)
-LATE = 1
+LATE = 2
 
 FLOPS = 2 * P * P * N + 2 * P * N * S
 

import concourse.mybir as mybir
from concourse.masks import make_identity

BF16, F32, U16 = mybir.dt.bfloat16, mybir.dt.float32, mybir.dt.uint16
MULT, ADD = mybir.AluOpType.mult, mybir.AluOpType.add
COPY = mybir.ActivationFunctionType.Copy

P = 128
S = 2048
N = 1024
BANK = 512
BLOCKS = N // P
BANKS = S // BANK
PIECES = (1, 3, 4)
LATE = 2

FLOPS = 2 * P * P * N + 2 * P * N * S


def tile_ourslayer2_kernel(tc, table, w2, city_mask, prov_mask, offs, out):
    nc = tc.nc
    with (
        tc.tile_pool(name="held", bufs=1) as held,
        tc.tile_pool(name="mask_pool", bufs=BLOCKS) as mask_pool,
        tc.tile_pool(name="work", bufs=3) as work,
        tc.tile_pool(name="stats", bufs=BLOCKS) as stats,
        tc.psum_pool(name="psum_h", bufs=2) as psum_h,
        tc.psum_pool(name="psum_held", bufs=1) as psum_held,
    ):
        table_sb = held.tile([P, S], BF16, name="table_sb")
        nc.sync.dma_start(table_sb[:], table)
        w2_sb = held.tile([P, P], BF16, name="w2_sb")
        nc.scalar.dma_start(w2_sb[:], w2)
        offsets = held.tile([P, N // 16], U16, name="offsets")
        nc.sync.dma_start(offsets[:], offs)
        city_blocks, prov_blocks = [], []
        for b in range(BLOCKS):
            city = mask_pool.tile([P, S], BF16, name="city")
            if b == 0:
                for half in range(2):
                    columns = slice(half * (S // 2), (half + 1) * (S // 2))
                    nc.sync.dma_start(city[:, columns], city_mask[0:P, columns])
            else:
                nc.sync.dma_start(city[:], city_mask[b * P : (b + 1) * P, :])
            prov = mask_pool.tile([P, S], BF16, name="prov")
            nc.sync.dma_start(prov[:], prov_mask[b * P : (b + 1) * P, :])
            city_blocks.append(city)
            prov_blocks.append(prov)

        identity = held.tile([P, P], BF16, name="identity")
        make_identity(nc, identity[:])

        hT_blocks = []
        for piece, count in enumerate(PIECES):
            first = len(hT_blocks)
            width = count * P
            h_ps = psum_h.tile([P, BANK], F32, name="h_ps", tag="h_ps")
            piece_offsets = offsets[:, first * (P // 16) : (first + count) * (P // 16)]
            nc.tensor.matmul(h_ps[:, 0:width], w2_sb[:], table_sb[:].indirect(piece_offsets), start=True, stop=True)
            h_bf = held.tile([P, width], BF16, name=f"h_bf{piece}")
            nc.scalar.copy(h_bf[:], h_ps[:, 0:width])
            if piece < len(PIECES) - 1:
                hT_ps = psum_held.tile([P, width], BF16, name=f"hT_ps{piece}")
            else:
                hT_ps = psum_h.tile([P, width], BF16, name="hT_ps", tag="h_ps")
            for k in range(count):
                nc.tensor.transpose(hT_ps[:, k * P : (k + 1) * P], h_bf[:, k * P : (k + 1) * P], identity[:])
                hT_blocks.append(hT_ps[:, k * P : (k + 1) * P])

        def weights_of(b, which, name):
            mask = (city_blocks, prov_blocks)[which][b]
            total = stats.tile([P, 1], F32, name=name + "_total")
            if which == 0 and b > 0:
                scalar_pass = work.tile([P, S], BF16, name="scalar_pass", bufs=2)
                nc.scalar.activation(scalar_pass[:], mask[:], COPY, accum_out=total[:])
                scalar_inv = stats.tile([P, 1], F32, name="scalar_inv")
                inv = scalar_inv[:]
            else:
                vector_tile = work.tile([P, S // 2 + 1], F32, name="vector_tile", bufs=2)
                unused = vector_tile[:, 0 : S // 2].bitcast(BF16)
                inv = vector_tile[:, S // 2 : S // 2 + 1]
                if b == 0 and which == 0:
                    half_total = stats.tile([P, 1], F32, name="half_total")
                    left, right = slice(0, S // 2), slice(S // 2, S)
                    nc.vector.tensor_scalar(
                        unused[:, left], mask[:, left], 1.0, None, MULT, ADD, accum_out=half_total[:]
                    )
                    nc.vector.tensor_scalar(
                        unused[:, right], mask[:, right], 1.0, half_total[:], MULT, ADD, accum_out=total[:]
                    )
                else:
                    nc.vector.tensor_scalar(unused, mask[:], 1.0, None, MULT, ADD, accum_out=total[:])
            nc.vector.reciprocal(inv, total[:])
            scaled = work.tile([P, P], BF16, name=name + "_scaled")
            nc.vector.tensor_scalar(scaled[:], hT_blocks[b], inv, None, MULT)
            return scaled, mask

        out_ps = [psum_held.tile([P, BANK], F32, name=f"out_ps{c}") for c in range(BANKS)]
        for b in range(BLOCKS - LATE):
            for which, name in enumerate(("city", "prov")):
                scaled, mask = weights_of(b, which, name)
                for c in range(BANKS):
                    nc.tensor.matmul(
                        out_ps[c][:], scaled[:], mask[:, c * BANK : (c + 1) * BANK], start=(b == 0 and which == 0), stop=False
                    )

        late = [
            weights_of(b, which, name)
            for b in range(BLOCKS - LATE, BLOCKS)
            for which, name in enumerate(("city", "prov"))
        ]
        out_sb = held.tile([P, S], F32, name="out_sb")
        for c in range(BANKS):
            columns = slice(c * BANK, (c + 1) * BANK)
            for k, (scaled, mask) in enumerate(late):
                nc.tensor.matmul(out_ps[c][:], scaled[:], mask[:, columns], start=False, stop=(k == len(late) - 1))
            if c % 2 == 0:
                nc.scalar.copy(out_sb[:, columns], out_ps[c][:])
            else:
                nc.vector.tensor_copy(out_sb[:, columns], out_ps[c][:])
            nc.sync.dma_start(out[:, columns], out_sb[:, columns])
